import numpy as np
import ml_dtypes


def mxq(x, axis, fmt="e4m3"):
    dtype, down = {"e4m3": (ml_dtypes.float8_e4m3fn, 7), "e5m2": (ml_dtypes.float8_e5m2, 14)}[fmt]
    v = np.moveaxis(np.asarray(x, np.float32).astype(ml_dtypes.bfloat16).astype(np.float64), axis, -1)
    blocks = v.reshape(v.shape[:-1] + (-1, 32))
    amax = np.abs(blocks).max(-1, keepdims=True)
    byte = np.maximum(np.where(amax > 0, np.frexp(amax)[1] - 1 + 127, 0) - down, 1)
    scale = np.exp2(byte - 127.0)
    codes = (blocks / scale).astype(np.float32).astype(dtype).astype(np.float64)
    return np.moveaxis((codes * scale).reshape(v.shape), -1, axis)


WIDE = False


def mx_kscale(k):
    if not WIDE:
        return np.ones(k)
    levels = np.array([10, -10, 5, -5, 0])
    if k % 512:
        return np.exp2(np.random.permutation(np.resize(levels, k // 32))).repeat(32)
    a = np.empty((k // 512, 16))
    for p in range(k // 512):
        a[p, :8] = np.random.permutation(np.resize(levels, 8))
        for g in range(8):
            far = levels[np.abs(levels - a[p, g]) >= 10]
            a[p, g + 8] = far[np.random.randint(len(far))]
    return np.exp2(a.ravel()).repeat(32)


BF16 = ml_dtypes.bfloat16


def bf(x):
    return np.asarray(x, np.float32).astype(BF16)


def f64(x):
    return np.asarray(x).astype(np.float64)


B, S, E, HID, H = 2, 128, 512, 1024, 8
DH = HID // H


def setup_inputs():
    t = mx_kscale(HID)
    kv_rms = np.hypot(6.0 * np.sqrt(S), 0.19 * S)
    return {"q_feat": bf(1.0 + 2.8 * np.random.standard_normal((B, H, S, DH))),
            "kv": bf(np.random.standard_normal((B, H, DH, DH)) * kv_rms * t.reshape(H, 1, DH)),
            "denom": bf(S * DH * (1.0 + 0.1 * np.random.standard_normal((B, H, 1, 1)))),
            "Wo": bf(np.random.standard_normal((HID, E)) * 4.0 / np.sqrt(HID) / t[:, None]),
            "bo": bf(np.random.standard_normal(E) * 0.1)}


def reference(q_feat, kv, denom, Wo, bo):
    qkv = f64(q_feat) @ f64(kv)
    ctx = qkv / f64(denom)
    ctx = ctx.transpose(0, 2, 1, 3).reshape(B, S, HID)
    return (mxq(ctx, 2, "e4m3") @ mxq(f64(Wo), 0, "e4m3")) + f64(bo)

@@ -1,0 +1,245 @@
+from contextlib import ExitStack
+
+import concourse.mybir as mybir
+from concourse.masks import make_identity
+
+BF16 = mybir.dt.bfloat16
+F32 = mybir.dt.float32
+U32 = mybir.dt.uint32
+U8 = mybir.dt.uint8
+FP8X4 = mybir.dt.float8_e4m3fn_x4
+MULT = mybir.AluOpType.mult
+ADD = mybir.AluOpType.add
+COPY = mybir.ActivationFunctionType.Copy
+
+P = 128
+B = 2
+H = 8
+S = 128
+DH = 128
+E = 512
+PACK = 4
+PASSES = H // PACK
+HALF = E // 2
+ROWS = 4
+RUNS = S // ROWS
+
+FLOPS = 2 * B * H * S * DH * DH + 2 * B * S * H * DH * E
+
+
+def tile_linearattention_pb_s_kernel(tc, q_feat, kv, denom, Wo, bo, out):
+    nc = tc.nc
+    with ExitStack() as ctx:
+        keep = ctx.enter_context(tc.tile_pool(name="keep", bufs=1))
+        psum_t = ctx.enter_context(tc.psum_pool(name="psum_t", bufs=2))
+        psum_c = ctx.enter_context(tc.psum_pool(name="psum_c", bufs=2))
+        psum_o = ctx.enter_context(tc.psum_pool(name="psum_o", bufs=1))
+        ctx.enter_context(tc.manual_schedule())
+
+        q_rows = [keep.tile([P, PASSES, ROWS, DH], BF16, name="q_rows%d" % b) for b in range(B)]
+        kv_sb = [keep.tile([P, H, DH], BF16, name="kv_sb%d" % b) for b in range(B)]
+        wo_raw = [keep.tile([P, PACK, E], BF16, name="wo_raw%d" % g) for g in range(PASSES)]
+        wo_view = Wo.rearrange("(g p t) n -> g p t n", t=PACK, p=P)
+
+        def load_q(b):
+            nc.sync.dma_start(
+                out=q_rows[b][:], in_=q_feat[b].rearrange("(g t) (u j) d -> (t u) g j d", t=PACK, j=ROWS)
+            )
+
+        def load_kv(b, g):
+            heads = slice(g * PACK, (g + 1) * PACK)
+            nc.sync.dma_start(out=kv_sb[b][:, heads, :], in_=kv[b, heads].rearrange("h d e -> d h e"))
+
+        def load_wo(g):
+            nc.sync.dma_start(out=wo_raw[g][:], in_=wo_view[g])
+
+        denom_all = keep.tile([P, B * H], BF16, name="denom_all")
+        bias_row = keep.tile([P, E], BF16, name="bias_row")
+        ones = keep.tile([P, P], BF16, name="ones")
+        nc.vector.memset(bias_row[:], 0.0)
+        nc.vector.memset(ones[:], 1.0)
+        load_q(0)
+        nc.scalar.dma_start(out=denom_all[:], in_=denom.rearrange("b h x y -> (b h x y)").partition_broadcast(P))
+        nc.scalar.dma_start(out=bias_row[0:1, :], in_=bo.unsqueeze(0))
+        load_kv(0, 0)
+        load_kv(0, 1)
+        load_wo(0)
+        load_q(1)
+        load_kv(1, 0)
+        load_kv(1, 1)
+        load_wo(1)
+
+        ident = keep.tile([P, P], BF16, name="ident")
+        make_identity(nc, ident[:])
+        ident_words = keep.tile([P, P], F32, name="ident_words")
+        make_identity(nc, ident_words[:])
+
+        recip = keep.tile([P, B * H], F32, name="recip")
+        nc.vector.reciprocal(out=recip[:], in_=denom_all[:])
+
+        bias_ps = psum_c.tile([P, E], F32, name="c_ps")
+        nc.tensor.matmul(bias_ps[:], lhsT=ones[:], rhs=bias_row[:], start=True, stop=True)
+        bias = keep.tile([P, E], F32, name="bias")
+        nc.scalar.copy(out=bias[:], in_=bias_ps[:])
+
+        t_ps = {}
+        c_ps = {}
+        w_ps = {}
+        q_t = {}
+        c_sb = {}
+        for b in range(B):
+            for g in range(PASSES):
+                q_t[b, g] = keep.tile([P, PACK, ROWS, RUNS], BF16, name="q_t%d%d" % (b, g))
+                c_sb[b, g] = keep.tile([P, PACK * DH], BF16, name="c_sb%d%d" % (b, g), align_bytes=64)
+        grouped = [keep.tile([P, PASSES, S, PACK], BF16, name="grouped%d" % b, align_bytes=64) for b in range(B)]
+        codes = [keep.tile([P, PASSES * S], U32, name="codes%d" % b, align_bytes=64) for b in range(B)]
+        scales = [keep.tile([P, PASSES * S], U8, name="scales%d" % b, align_bytes=64) for b in range(B)]
+        wo_grouped = [keep.tile([P, E, PACK], BF16, name="wo_grouped%d" % g, align_bytes=64) for g in range(PASSES)]
+        wo_codes = [keep.tile([P, E], U32, name="wo_codes%d" % g, align_bytes=64) for g in range(PASSES)]
+        wo_scales = [keep.tile([P, E], U8, name="wo_scales%d" % g, align_bytes=64) for g in range(PASSES)]
+
+        def copy(engine, out, in_):
+            if engine is nc.scalar:
+                nc.scalar.copy(out=out, in_=in_)
+            else:
+                engine.tensor_copy(out=out, in_=in_)
+
+        def transpose_q(b, g):
+            t_ps[b, g] = psum_t.tile([P, ROWS, P], BF16, name="t_ps")
+            for j in range(ROWS):
+                nc.tensor.transpose(t_ps[b, g][:, j, :], q_rows[b][:, g, j, :], ident[:])
+
+        def copy_q(engine, b, g):
+            copy(engine, q_t[b, g][:], t_ps[b, g][:].rearrange("d j (t u) -> d t j u", u=RUNS))
+
+        def first_matmul(b, g):
+            c_ps[b, g] = psum_c.tile([P, PACK, DH], F32, name="c_ps")
+            for t in range(PACK):
+                nc.tensor.matmul(
+                    c_ps[b, g][:, t, :],
+                    lhsT=q_t[b, g][:, t, :, :].rearrange("d j u -> d (j u)"),
+                    rhs=kv_sb[b][:, g * PACK + t, :],
+                    start=True,
+                    stop=True,
+                )
+
+        def divide(engine, b, g):
+            first = b * H + g * PACK
+            if engine is nc.scalar:
+                for t in range(PACK):
+                    nc.scalar.activation(
+                        out=c_sb[b, g][:, t * DH : (t + 1) * DH],
+                        in_=c_ps[b, g][:, t, :],
+                        func=COPY,
+                        scale=recip[:, first + t : first + t + 1],
+                    )
+            else:
+                nc.vector.tensor_tensor(
+                    out=c_sb[b, g][:].rearrange("p (t e) -> p t e", t=PACK),
+                    in0=c_ps[b, g][:],
+                    in1=recip[:, first : first + PACK].unsqueeze(2).to_broadcast([P, PACK, DH]),
+                    op=MULT,
+                )
+
+        def transpose_c(b, g):
+            w_ps[b, g] = psum_t.tile([P, 2, S], F32, name="t_ps")
+            words = c_sb[b, g][:].bitcast(F32)
+            for u in range(2):
+                nc.tensor.transpose(w_ps[b, g][:, u, :], words[:, u::2], ident_words[:])
+
+        def copy_c(engine, b, g):
+            copy(
+                engine,
+                grouped[b][:, g, :, :].rearrange("p s t -> p (s t)").bitcast(F32).rearrange("p (u j w) -> p u j w", j=ROWS, w=2),
+                w_ps[b, g][:].rearrange("p w (j u) -> p u j w", j=ROWS),
+            )
+
+        def quantise_c(b, g):
+            cols = slice(g * S, (g + 1) * S)
+            nc.vector.quantize_mx(
+                out=codes[b][:, cols].bitcast(FP8X4),
+                scales=scales[b][:, cols],
+                in_=grouped[b][:, g, :, :].rearrange("p s t -> p (s t)"),
+            )
+
+        def group_wo(engine, g, lo, hi):
+            dst = wo_grouped[g][:, lo:hi, :].rearrange("p (c i) t -> p c t i", i=4)
+            src = wo_raw[g][:, :, lo:hi].rearrange("p t (c i) -> p c t i", i=4)
+            copy(engine, dst, src)
+
+        def quantise_wo(g, lo, hi):
+            nc.vector.quantize_mx(
+                out=wo_codes[g][:, lo:hi].bitcast(FP8X4),
+                scales=wo_scales[g][:, lo:hi],
+                in_=wo_grouped[g][:, lo:hi, :].rearrange("p n t -> p (n t)"),
+            )
+
+        o_ps = {}
+
+        def second_matmul(b, g, half):
+            cols = slice(half * HALF, (half + 1) * HALF)
+            if g == 0:
+                o_ps[b, half] = psum_o.tile([P, HALF], F32, name="o_ps%d%d" % (b, half))
+            nc.tensor.matmul_mx(
+                out=o_ps[b, half][:],
+                lhsT=codes[b][:, g * S : (g + 1) * S].bitcast(FP8X4),
+                lhsT_scale=scales[b][:, g * S : (g + 1) * S],
+                rhs=wo_codes[g][:, cols].bitcast(FP8X4),
+                rhs_scale=wo_scales[g][:, cols],
+                start=(g == 0),
+                stop=(g == PASSES - 1),
+            )
+
+        def finish(b, half):
+            cols = slice(half * HALF, (half + 1) * HALF)
+            result = keep.tile([P, HALF], F32, name="result%d%d" % (b, half))
+            nc.vector.tensor_tensor(out=result[:], in0=o_ps[b, half][:], in1=bias[:, cols], op=ADD)
+            nc.sync.dma_start(out=out[b][:, cols], in_=result[:])
+
+        S_, V_ = nc.scalar, nc.vector
+        transpose_q(0, 0)
+        copy_q(S_, 0, 0)
+        transpose_q(0, 1)
+        copy_q(S_, 0, 1)
+        first_matmul(0, 0)
+        divide(V_, 0, 0)
+        first_matmul(0, 1)
+        divide(V_, 0, 1)
+        transpose_c(0, 0)
+        copy_c(S_, 0, 0)
+        transpose_c(0, 1)
+        copy_c(S_, 0, 1)
+        group_wo(V_, 0, 0, E)
+        transpose_q(1, 0)
+        copy_q(S_, 1, 0)
+        transpose_q(1, 1)
+        copy_q(S_, 1, 1)
+        quantise_c(0, 0)
+        quantise_c(0, 1)
+        quantise_wo(0, 0, E)
+        first_matmul(1, 0)
+        divide(S_, 1, 0)
+        first_matmul(1, 1)
+        divide(S_, 1, 1)
+        transpose_c(1, 0)
+        copy_c(S_, 1, 0)
+        transpose_c(1, 1)
+        copy_c(S_, 1, 1)
+        group_wo(V_, 1, 0, HALF)
+        group_wo(V_, 1, HALF, E)
+        quantise_wo(1, 0, HALF)
+        quantise_c(1, 0)
+        quantise_c(1, 1)
+        for half in range(2):
+            second_matmul(0, 0, half)
+        for half in range(2):
+            second_matmul(1, 0, half)
+        second_matmul(0, 1, 0)
+        second_matmul(1, 1, 0)
+        quantise_wo(1, HALF, E)
+        second_matmul(0, 1, 1)
+        second_matmul(1, 1, 1)
+        finish(0, 0)
+        finish(1, 0)
+        finish(0, 1)
+        finish(1, 1)

@@ -31,9 +31,7 @@ def tile_linearattention_pb_s_kernel(tc, q_feat, kv, denom, Wo, bo, out):
     nc = tc.nc
     with ExitStack() as ctx:
         keep = ctx.enter_context(tc.tile_pool(name="keep", bufs=1))
-        psum_t = ctx.enter_context(tc.psum_pool(name="psum_t", bufs=2))
-        psum_c = ctx.enter_context(tc.psum_pool(name="psum_c", bufs=2))
-        psum_o = ctx.enter_context(tc.psum_pool(name="psum_o", bufs=1))
+        psum = ctx.enter_context(tc.psum_pool(name="psum", bufs=8))
         ctx.enter_context(tc.manual_schedule())
 
         q_rows = [keep.tile([P, PASSES, ROWS, DH], BF16, name="q_rows%d" % b) for b in range(B)]
@@ -41,33 +39,39 @@ def tile_linearattention_pb_s_kernel(tc, q_feat, kv, denom, Wo, bo, out):
         wo_raw = [keep.tile([P, PACK, E], BF16, name="wo_raw%d" % g) for g in range(PASSES)]
         wo_view = Wo.rearrange("(g p t) n -> g p t n", t=PACK, p=P)
 
-        def load_q(b):
+        def load_q(b, g):
+            heads = slice(g * PACK, (g + 1) * PACK)
             nc.sync.dma_start(
-                out=q_rows[b][:], in_=q_feat[b].rearrange("(g t) (u j) d -> (t u) g j d", t=PACK, j=ROWS)
+                out=q_rows[b][:, g, :, :], in_=q_feat[b, heads].rearrange("t (u j) d -> (t u) j d", j=ROWS)
             )
 
         def load_kv(b, g):
             heads = slice(g * PACK, (g + 1) * PACK)
             nc.sync.dma_start(out=kv_sb[b][:, heads, :], in_=kv[b, heads].rearrange("h d e -> d h e"))
 
-        def load_wo(g):
-            nc.sync.dma_start(out=wo_raw[g][:], in_=wo_view[g])
+        def load_wo(g, half):
+            cols = slice(half * HALF, (half + 1) * HALF)
+            nc.sync.dma_start(out=wo_raw[g][:, :, cols], in_=wo_view[g][:, :, cols])
 
         denom_all = keep.tile([P, B * H], BF16, name="denom_all")
         bias_row = keep.tile([P, E], BF16, name="bias_row")
         ones = keep.tile([P, P], BF16, name="ones")
         nc.vector.memset(bias_row[:], 0.0)
         nc.vector.memset(ones[:], 1.0)
-        load_q(0)
+        load_q(0, 0)
         nc.scalar.dma_start(out=denom_all[:], in_=denom.rearrange("b h x y -> (b h x y)").partition_broadcast(P))
         nc.scalar.dma_start(out=bias_row[0:1, :], in_=bo.unsqueeze(0))
         load_kv(0, 0)
+        load_q(0, 1)
         load_kv(0, 1)
-        load_wo(0)
-        load_q(1)
+        load_q(1, 0)
+        load_wo(0, 0)
+        load_q(1, 1)
         load_kv(1, 0)
         load_kv(1, 1)
-        load_wo(1)
+        load_wo(0, 1)
+        load_wo(1, 0)
+        load_wo(1, 1)
 
         ident = keep.tile([P, P], BF16, name="ident")
         make_identity(nc, ident[:])
@@ -77,10 +81,12 @@ def tile_linearattention_pb_s_kernel(tc, q_feat, kv, denom, Wo, bo, out):
         recip = keep.tile([P, B * H], F32, name="recip")
         nc.vector.reciprocal(out=recip[:], in_=denom_all[:])
 
-        bias_ps = psum_c.tile([P, E], F32, name="c_ps")
-        nc.tensor.matmul(bias_ps[:], lhsT=ones[:], rhs=bias_row[:], start=True, stop=True)
         bias = keep.tile([P, E], F32, name="bias")
-        nc.scalar.copy(out=bias[:], in_=bias_ps[:])
+
+        def spread_bias():
+            bias_ps = psum.tile([P, E], F32, name="bank")
+            nc.tensor.matmul(bias_ps[:], lhsT=ones[:], rhs=bias_row[:], start=True, stop=True)
+            return bias_ps
 
         t_ps = {}
         c_ps = {}
@@ -105,7 +111,7 @@ def tile_linearattention_pb_s_kernel(tc, q_feat, kv, denom, Wo, bo, out):
                 engine.tensor_copy(out=out, in_=in_)
 
         def transpose_q(b, g):
-            t_ps[b, g] = psum_t.tile([P, ROWS, P], BF16, name="t_ps")
+            t_ps[b, g] = psum.tile([P, ROWS, P], BF16, name="bank")
             for j in range(ROWS):
                 nc.tensor.transpose(t_ps[b, g][:, j, :], q_rows[b][:, g, j, :], ident[:])
 
@@ -113,7 +119,7 @@ def tile_linearattention_pb_s_kernel(tc, q_feat, kv, denom, Wo, bo, out):
             copy(engine, q_t[b, g][:], t_ps[b, g][:].rearrange("d j (t u) -> d t j u", u=RUNS))
 
         def first_matmul(b, g):
-            c_ps[b, g] = psum_c.tile([P, PACK, DH], F32, name="c_ps")
+            c_ps[b, g] = psum.tile([P, PACK, DH], F32, name="bank")
             for t in range(PACK):
                 nc.tensor.matmul(
                     c_ps[b, g][:, t, :],
@@ -142,7 +148,7 @@ def tile_linearattention_pb_s_kernel(tc, q_feat, kv, denom, Wo, bo, out):
                 )
 
         def transpose_c(b, g):
-            w_ps[b, g] = psum_t.tile([P, 2, S], F32, name="t_ps")
+            w_ps[b, g] = psum.tile([P, 2, S], F32, name="bank")
             words = c_sb[b, g][:].bitcast(F32)
             for u in range(2):
                 nc.tensor.transpose(w_ps[b, g][:, u, :], words[:, u::2], ident_words[:])
@@ -179,7 +185,7 @@ def tile_linearattention_pb_s_kernel(tc, q_feat, kv, denom, Wo, bo, out):
         def second_matmul(b, g, half):
             cols = slice(half * HALF, (half + 1) * HALF)
             if g == 0:
-                o_ps[b, half] = psum_o.tile([P, HALF], F32, name="o_ps%d%d" % (b, half))
+                o_ps[b, half] = psum.tile([P, HALF], F32, name="bank")
             nc.tensor.matmul_mx(
                 out=o_ps[b, half][:],
                 lhsT=codes[b][:, g * S : (g + 1) * S].bitcast(FP8X4),
@@ -198,41 +204,45 @@ def tile_linearattention_pb_s_kernel(tc, q_feat, kv, denom, Wo, bo, out):
 
         S_, V_ = nc.scalar, nc.vector
         transpose_q(0, 0)
-        copy_q(S_, 0, 0)
+        copy_q(V_, 0, 0)
         transpose_q(0, 1)
-        copy_q(S_, 0, 1)
         first_matmul(0, 0)
-        divide(V_, 0, 0)
+        copy_q(V_, 0, 1)
+        divide(S_, 0, 0)
         first_matmul(0, 1)
-        divide(V_, 0, 1)
+        transpose_q(1, 0)
         transpose_c(0, 0)
+        copy_q(V_, 1, 0)
+        divide(S_, 0, 1)
+        transpose_q(1, 1)
+        group_wo(V_, 0, 0, HALF)
         copy_c(S_, 0, 0)
         transpose_c(0, 1)
-        copy_c(S_, 0, 1)
-        group_wo(V_, 0, 0, E)
-        transpose_q(1, 0)
-        copy_q(S_, 1, 0)
-        transpose_q(1, 1)
-        copy_q(S_, 1, 1)
-        quantise_c(0, 0)
-        quantise_c(0, 1)
-        quantise_wo(0, 0, E)
+        copy_q(V_, 1, 1)
         first_matmul(1, 0)
+        copy_c(S_, 0, 1)
+        quantise_wo(0, 0, HALF)
         divide(S_, 1, 0)
         first_matmul(1, 1)
-        divide(S_, 1, 1)
         transpose_c(1, 0)
+        divide(V_, 1, 1)
+        quantise_c(0, 0)
+        quantise_c(0, 1)
         copy_c(S_, 1, 0)
+        group_wo(V_, 0, HALF, E)
         transpose_c(1, 1)
         copy_c(S_, 1, 1)
+        bias_ps = spread_bias()
         group_wo(V_, 1, 0, HALF)
-        group_wo(V_, 1, HALF, E)
-        quantise_wo(1, 0, HALF)
+        group_wo(S_, 1, HALF, 416)
+        quantise_wo(0, HALF, E)
         quantise_c(1, 0)
         quantise_c(1, 1)
+        group_wo(V_, 1, 416, E)
+        quantise_wo(1, 0, HALF)
+        nc.scalar.copy(out=bias[:], in_=bias_ps[:])
         for half in range(2):
             second_matmul(0, 0, half)
-        for half in range(2):
             second_matmul(1, 0, half)
         second_matmul(0, 1, 0)
         second_matmul(1, 1, 0)

@@ -39,39 +39,43 @@ def tile_linearattention_pb_s_kernel(tc, q_feat, kv, denom, Wo, bo, out):
         wo_raw = [keep.tile([P, PACK, E], BF16, name="wo_raw%d" % g) for g in range(PASSES)]
         wo_view = Wo.rearrange("(g p t) n -> g p t n", t=PACK, p=P)
 
-        def load_q(b, g):
-            heads = slice(g * PACK, (g + 1) * PACK)
-            nc.sync.dma_start(
-                out=q_rows[b][:, g, :, :], in_=q_feat[b, heads].rearrange("t (u j) d -> (t u) j d", j=ROWS)
-            )
+        def load_q(b, g=None):
+            if g is None:
+                view = q_feat[b].rearrange("(g t) (u j) d -> (t u) g j d", t=PACK, j=ROWS)
+                nc.sync.dma_start(out=q_rows[b][:], in_=view)
+            else:
+                heads = slice(g * PACK, (g + 1) * PACK)
+                view = q_feat[b, heads].rearrange("t (u j) d -> (t u) j d", j=ROWS)
+                nc.sync.dma_start(out=q_rows[b][:, g, :, :], in_=view)
 
-        def load_kv(b, g):
-            heads = slice(g * PACK, (g + 1) * PACK)
+        def load_kv(b, g=None):
+            heads = slice(0, H) if g is None else slice(g * PACK, (g + 1) * PACK)
             nc.sync.dma_start(out=kv_sb[b][:, heads, :], in_=kv[b, heads].rearrange("h d e -> d h e"))
 
-        def load_wo(g, half):
-            cols = slice(half * HALF, (half + 1) * HALF)
+        def load_wo(g, half=None):
+            cols = slice(0, E) if half is None else slice(half * HALF, (half + 1) * HALF)
             nc.sync.dma_start(out=wo_raw[g][:, :, cols], in_=wo_view[g][:, :, cols])
 
+        def load_denom():
+            view = denom.rearrange("b h x y -> (b h x y)").partition_broadcast(P)
+            nc.scalar.dma_start(out=denom_all[:], in_=view)
+
+        def load_bo():
+            nc.scalar.dma_start(out=bo_cols[:], in_=bo.rearrange("(p c) -> p c", p=P))
+
         denom_all = keep.tile([P, B * H], BF16, name="denom_all")
-        bias_row = keep.tile([P, E], BF16, name="bias_row")
-        ones = keep.tile([P, P], BF16, name="ones")
-        nc.vector.memset(bias_row[:], 0.0)
-        nc.vector.memset(ones[:], 1.0)
+        bo_cols = keep.tile([P, E // P], BF16, name="bo_cols")
         load_q(0, 0)
-        nc.scalar.dma_start(out=denom_all[:], in_=denom.rearrange("b h x y -> (b h x y)").partition_broadcast(P))
-        nc.scalar.dma_start(out=bias_row[0:1, :], in_=bo.unsqueeze(0))
+        load_denom()
+        load_bo()
         load_kv(0, 0)
         load_q(0, 1)
         load_kv(0, 1)
-        load_q(1, 0)
-        load_wo(0, 0)
-        load_q(1, 1)
+        load_wo(0)
+        load_q(1)
         load_kv(1, 0)
         load_kv(1, 1)
-        load_wo(0, 1)
-        load_wo(1, 0)
-        load_wo(1, 1)
+        load_wo(1)
 
         ident = keep.tile([P, P], BF16, name="ident")
         make_identity(nc, ident[:])
@@ -81,12 +85,16 @@ def tile_linearattention_pb_s_kernel(tc, q_feat, kv, denom, Wo, bo, out):
         recip = keep.tile([P, B * H], F32, name="recip")
         nc.vector.reciprocal(out=recip[:], in_=denom_all[:])
 
-        bias = keep.tile([P, E], F32, name="bias")
+        bias = keep.tile([P, E], BF16, name="bias")
 
         def spread_bias():
-            bias_ps = psum.tile([P, E], F32, name="bank")
-            nc.tensor.matmul(bias_ps[:], lhsT=ones[:], rhs=bias_row[:], start=True, stop=True)
+            bias_ps = psum.tile([P, E // P, P], BF16, name="bank")
+            for c in range(E // P):
+                nc.tensor.transpose(bias_ps[:, c, :], bo_cols[:, c : c + 1].to_broadcast([P, P]), ident[:])
             return bias_ps
+
+        def copy_bias(engine, bias_ps):
+            copy(engine, bias[:].rearrange("m (p c) -> m p c", p=P), bias_ps[:].rearrange("m c p -> m p c"))
 
         t_ps = {}
         c_ps = {}
@@ -210,46 +218,46 @@ def tile_linearattention_pb_s_kernel(tc, q_feat, kv, denom, Wo, bo, out):
         copy_q(V_, 0, 1)
         divide(S_, 0, 0)
         first_matmul(0, 1)
-        transpose_q(1, 0)
+        group_wo(S_, 0, 384, E)
+        divide(V_, 0, 1)
         transpose_c(0, 0)
-        copy_q(V_, 1, 0)
-        divide(S_, 0, 1)
-        transpose_q(1, 1)
-        group_wo(V_, 0, 0, HALF)
+        transpose_q(1, 0)
+        group_wo(V_, 0, 0, 384)
         copy_c(S_, 0, 0)
+        transpose_q(1, 1)
         transpose_c(0, 1)
-        copy_q(V_, 1, 1)
+        copy_q(V_, 1, 0)
+        copy_q(S_, 1, 1)
+        quantise_c(0, 0)
+        quantise_wo(0, 0, E)
         first_matmul(1, 0)
         copy_c(S_, 0, 1)
-        quantise_wo(0, 0, HALF)
-        divide(S_, 1, 0)
         first_matmul(1, 1)
-        transpose_c(1, 0)
-        divide(V_, 1, 1)
-        quantise_c(0, 0)
         quantise_c(0, 1)
-        copy_c(S_, 1, 0)
-        group_wo(V_, 0, HALF, E)
-        transpose_c(1, 1)
-        copy_c(S_, 1, 1)
         bias_ps = spread_bias()
+        divide(V_, 1, 0)
+        divide(S_, 1, 1)
         group_wo(V_, 1, 0, HALF)
-        group_wo(S_, 1, HALF, 416)
-        quantise_wo(0, HALF, E)
-        quantise_c(1, 0)
-        quantise_c(1, 1)
-        group_wo(V_, 1, 416, E)
+        transpose_c(1, 0)
+        transpose_c(1, 1)
         quantise_wo(1, 0, HALF)
-        nc.scalar.copy(out=bias[:], in_=bias_ps[:])
-        for half in range(2):
-            second_matmul(0, 0, half)
-            second_matmul(1, 0, half)
+        copy_c(S_, 1, 0)
+        second_matmul(0, 0, 0)
+        group_wo(V_, 1, 384, E)
+        group_wo(S_, 1, HALF, 384)
+        quantise_c(1, 0)
+        copy_c(S_, 1, 1)
+        second_matmul(1, 0, 0)
+        second_matmul(0, 0, 1)
+        copy_bias(S_, bias_ps)
+        second_matmul(1, 0, 1)
+        quantise_c(1, 1)
         second_matmul(0, 1, 0)
-        second_matmul(1, 1, 0)
         quantise_wo(1, HALF, E)
-        second_matmul(0, 1, 1)
-        second_matmul(1, 1, 1)
+        second_matmul(1, 1, 0)
         finish(0, 0)
+        second_matmul(0, 1, 1)
         finish(1, 0)
+        second_matmul(1, 1, 1)
         finish(0, 1)
         finish(1, 1)

@@ -80,7 +80,7 @@ def tile_linearattention_pb_s_kernel(tc, q_feat, kv, denom, Wo, bo, out):
         ident = keep.tile([P, P], BF16, name="ident")
         make_identity(nc, ident[:])
         ident_words = keep.tile([P, P], F32, name="ident_words")
-        make_identity(nc, ident_words[:])
+        nc.vector.tensor_copy(out=ident_words[:], in_=ident[:])
 
         recip = keep.tile([P, B * H], F32, name="recip")
         nc.vector.reciprocal(out=recip[:], in_=denom_all[:])
@@ -115,6 +115,8 @@ def tile_linearattention_pb_s_kernel(tc, q_feat, kv, denom, Wo, bo, out):
         def copy(engine, out, in_):
             if engine is nc.scalar:
                 nc.scalar.copy(out=out, in_=in_)
+            elif engine is nc.gpsimd:
+                nc.gpsimd.tensor_scalar(out=out, in0=in_, scalar1=1.0, scalar2=0.0, op0=MULT, op1=ADD)
             else:
                 engine.tensor_copy(out=out, in_=in_)
 
@@ -168,12 +170,12 @@ def tile_linearattention_pb_s_kernel(tc, q_feat, kv, denom, Wo, bo, out):
                 w_ps[b, g][:].rearrange("p w (j u) -> p u j w", j=ROWS),
             )
 
-        def quantise_c(b, g):
-            cols = slice(g * S, (g + 1) * S)
+        def quantise_c(b, g=None):
+            lo, hi = (0, PASSES) if g is None else (g, g + 1)
             nc.vector.quantize_mx(
-                out=codes[b][:, cols].bitcast(FP8X4),
-                scales=scales[b][:, cols],
-                in_=grouped[b][:, g, :, :].rearrange("p s t -> p (s t)"),
+                out=codes[b][:, lo * S : hi * S].bitcast(FP8X4),
+                scales=scales[b][:, lo * S : hi * S],
+                in_=grouped[b][:, lo:hi, :, :].rearrange("p g s t -> p (g s t)"),
             )
 
         def group_wo(engine, g, lo, hi):
@@ -190,74 +192,71 @@ def tile_linearattention_pb_s_kernel(tc, q_feat, kv, denom, Wo, bo, out):
 
         o_ps = {}
 
-        def second_matmul(b, g, half):
-            cols = slice(half * HALF, (half + 1) * HALF)
+        def second_matmul(b, g, lo, hi):
             if g == 0:
-                o_ps[b, half] = psum.tile([P, HALF], F32, name="bank")
+                o_ps[b, lo] = psum.tile([P, hi - lo], F32, name="bank")
             nc.tensor.matmul_mx(
-                out=o_ps[b, half][:],
+                out=o_ps[b, lo][:],
                 lhsT=codes[b][:, g * S : (g + 1) * S].bitcast(FP8X4),
                 lhsT_scale=scales[b][:, g * S : (g + 1) * S],
-                rhs=wo_codes[g][:, cols].bitcast(FP8X4),
-                rhs_scale=wo_scales[g][:, cols],
+                rhs=wo_codes[g][:, lo:hi].bitcast(FP8X4),
+                rhs_scale=wo_scales[g][:, lo:hi],
                 start=(g == 0),
                 stop=(g == PASSES - 1),
             )
 
-        def finish(b, half):
-            cols = slice(half * HALF, (half + 1) * HALF)
-            result = keep.tile([P, HALF], F32, name="result%d%d" % (b, half))
-            nc.vector.tensor_tensor(out=result[:], in0=o_ps[b, half][:], in1=bias[:, cols], op=ADD)
-            nc.sync.dma_start(out=out[b][:, cols], in_=result[:])
+        def finish(b, lo, hi):
+            result = keep.tile([P, hi - lo], F32, name="result%d%d" % (b, lo))
+            nc.vector.tensor_tensor(out=result[:], in0=o_ps[b, lo][:], in1=bias[:, lo:hi], op=ADD)
+            nc.sync.dma_start(out=out[b][:, lo:hi], in_=result[:])
 
-        S_, V_ = nc.scalar, nc.vector
+        S_, V_, G_ = nc.scalar, nc.vector, nc.gpsimd
         transpose_q(0, 0)
         copy_q(V_, 0, 0)
         transpose_q(0, 1)
         first_matmul(0, 0)
         copy_q(V_, 0, 1)
+        bias_ps = spread_bias()
         divide(S_, 0, 0)
         first_matmul(0, 1)
+        group_wo(G_, 0, HALF, 384)
         group_wo(S_, 0, 384, E)
-        divide(V_, 0, 1)
         transpose_c(0, 0)
+        divide(V_, 0, 1)
+        copy_bias(S_, bias_ps)
         transpose_q(1, 0)
-        group_wo(V_, 0, 0, 384)
-        copy_c(S_, 0, 0)
+        group_wo(V_, 0, 0, HALF)
         transpose_q(1, 1)
-        transpose_c(0, 1)
+        copy_c(S_, 0, 0)
         copy_q(V_, 1, 0)
+        transpose_c(0, 1)
         copy_q(S_, 1, 1)
-        quantise_c(0, 0)
         quantise_wo(0, 0, E)
         first_matmul(1, 0)
         copy_c(S_, 0, 1)
+        group_wo(G_, 1, HALF, 384)
         first_matmul(1, 1)
-        quantise_c(0, 1)
-        bias_ps = spread_bias()
         divide(V_, 1, 0)
         divide(S_, 1, 1)
-        group_wo(V_, 1, 0, HALF)
+        quantise_c(0)
         transpose_c(1, 0)
-        transpose_c(1, 1)
-        quantise_wo(1, 0, HALF)
+        group_wo(V_, 1, 0, HALF)
         copy_c(S_, 1, 0)
-        second_matmul(0, 0, 0)
+        transpose_c(1, 1)
         group_wo(V_, 1, 384, E)
-        group_wo(S_, 1, HALF, 384)
-        quantise_c(1, 0)
+        second_matmul(0, 0, 0, HALF)
+        quantise_wo(1, 0, HALF)
+        second_matmul(0, 0, HALF, E)
         copy_c(S_, 1, 1)
-        second_matmul(1, 0, 0)
-        second_matmul(0, 0, 1)
-        copy_bias(S_, bias_ps)
-        second_matmul(1, 0, 1)
-        quantise_c(1, 1)
-        second_matmul(0, 1, 0)
         quantise_wo(1, HALF, E)
-        second_matmul(1, 1, 0)
-        finish(0, 0)
-        second_matmul(0, 1, 1)
-        finish(1, 0)
-        second_matmul(1, 1, 1)
-        finish(0, 1)
-        finish(1, 1)
+        second_matmul(0, 1, 0, HALF)
+        quantise_c(1)
+        second_matmul(0, 1, HALF, E)
+        finish(0, 0, HALF)
+        second_matmul(1, 0, 0, HALF)
+        finish(0, HALF, E)
+        second_matmul(1, 1, 0, HALF)
+        second_matmul(1, 0, HALF, E)
+        second_matmul(1, 1, HALF, E)
+        finish(1, 0, HALF)
+        finish(1, HALF, E)

@@ -71,8 +71,8 @@ def tile_linearattention_pb_s_kernel(tc, q_feat, kv, denom, Wo, bo, out):
         load_kv(0, 0)
         load_q(0, 1)
         load_kv(0, 1)
-        load_wo(0)
         load_q(1)
+        load_wo(0)
         load_kv(1, 0)
         load_kv(1, 1)
         load_wo(1)
@@ -217,45 +217,45 @@ def tile_linearattention_pb_s_kernel(tc, q_feat, kv, denom, Wo, bo, out):
         first_matmul(0, 0)
         copy_q(V_, 0, 1)
         bias_ps = spread_bias()
-        divide(S_, 0, 0)
+        divide(V_, 0, 0)
         first_matmul(0, 1)
-        group_wo(G_, 0, HALF, 384)
-        group_wo(S_, 0, 384, E)
-        transpose_c(0, 0)
-        divide(V_, 0, 1)
         copy_bias(S_, bias_ps)
         transpose_q(1, 0)
-        group_wo(V_, 0, 0, HALF)
+        divide(V_, 0, 1)
+        group_wo(G_, 0, HALF, 384)
         transpose_q(1, 1)
-        copy_c(S_, 0, 0)
-        copy_q(V_, 1, 0)
+        copy_q(S_, 1, 0)
+        group_wo(V_, 0, 0, HALF)
+        transpose_c(0, 0)
         transpose_c(0, 1)
         copy_q(S_, 1, 1)
-        quantise_wo(0, 0, E)
+        group_wo(V_, 0, 384, E)
         first_matmul(1, 0)
-        copy_c(S_, 0, 1)
-        group_wo(G_, 1, HALF, 384)
+        copy_c(S_, 0, 0)
         first_matmul(1, 1)
         divide(V_, 1, 0)
+        copy_c(S_, 0, 1)
+        group_wo(G_, 1, HALF, 384)
         divide(S_, 1, 1)
-        quantise_c(0)
+        quantise_wo(0, 0, E)
         transpose_c(1, 0)
+        group_wo(S_, 1, 384, E)
         group_wo(V_, 1, 0, HALF)
-        copy_c(S_, 1, 0)
         transpose_c(1, 1)
-        group_wo(V_, 1, 384, E)
-        second_matmul(0, 0, 0, HALF)
-        quantise_wo(1, 0, HALF)
-        second_matmul(0, 0, HALF, E)
+        copy_c(S_, 1, 0)
+        quantise_c(0)
         copy_c(S_, 1, 1)
+        quantise_wo(1, 0, HALF)
+        second_matmul(0, 0, 0, HALF)
         quantise_wo(1, HALF, E)
-        second_matmul(0, 1, 0, HALF)
+        second_matmul(0, 0, HALF, E)
         quantise_c(1)
+        second_matmul(0, 1, 0, HALF)
         second_matmul(0, 1, HALF, E)
         finish(0, 0, HALF)
         second_matmul(1, 0, 0, HALF)
-        finish(0, HALF, E)
         second_matmul(1, 1, 0, HALF)
+        finish(0, HALF, E)
         second_matmul(1, 0, HALF, E)
         second_matmul(1, 1, HALF, E)
         finish(1, 0, HALF)

@@ -179,9 +179,16 @@ def tile_linearattention_pb_s_kernel(tc, q_feat, kv, denom, Wo, bo, out):
             )
 
         def group_wo(engine, g, lo, hi):
-            dst = wo_grouped[g][:, lo:hi, :].rearrange("p (c i) t -> p c t i", i=4)
-            src = wo_raw[g][:, :, lo:hi].rearrange("p t (c i) -> p c t i", i=4)
-            copy(engine, dst, src)
+            dst = wo_grouped[g][:, lo:hi, :]
+            src = wo_raw[g][:, :, lo:hi]
+            if engine is nc.gpsimd:
+                copy(engine, dst, src.rearrange("p t n -> p n t"))
+            else:
+                copy(
+                    engine,
+                    dst.rearrange("p (c i) t -> p c t i", i=4),
+                    src.rearrange("p t (c i) -> p c t i", i=4),
+                )
 
         def quantise_wo(g, lo, hi):
             nc.vector.quantize_mx(

@@ -19,6 +19,7 @@ S = 128
 DH = 128
 E = 512
 PACK = 4
+PAIRS = 2
 PASSES = H // PACK
 HALF = E // 2
 ROWS = 4
@@ -57,14 +58,17 @@ def tile_linearattention_pb_s_kernel(tc, q_feat, kv, denom, Wo, bo, out):
             nc.sync.dma_start(out=wo_raw[g][:, :, cols], in_=wo_view[g][:, :, cols])
 
         def load_denom():
-            view = denom.rearrange("b h x y -> (b h x y)").partition_broadcast(P)
-            nc.scalar.dma_start(out=denom_all[:], in_=view)
+            nc.scalar.dma_start(out=denom_col[0 : B * H, 0:1], in_=denom.rearrange("b h x y -> (b h) (x y)"))
 
         def load_bo():
-            nc.scalar.dma_start(out=bo_cols[:], in_=bo.rearrange("(p c) -> p c", p=P))
+            nc.scalar.dma_start(out=bias_row[0:1, :], in_=bo.unsqueeze(0))
 
-        denom_all = keep.tile([P, B * H], BF16, name="denom_all")
-        bo_cols = keep.tile([P, E // P], BF16, name="bo_cols")
+        denom_col = keep.tile([P, 2], BF16, name="denom_col")
+        nc.vector.memset(denom_col[:], 0.0)
+        bias_row = keep.tile([P, E], BF16, name="bias_row")
+        nc.vector.memset(bias_row[:], 0.0)
+        ones = keep.tile([P, P], BF16, name="ones")
+        nc.vector.memset(ones[:], 1.0)
         load_q(0, 0)
         load_denom()
         load_bo()
@@ -83,18 +87,21 @@ def tile_linearattention_pb_s_kernel(tc, q_feat, kv, denom, Wo, bo, out):
         nc.vector.tensor_copy(out=ident_words[:], in_=ident[:])
 
         recip = keep.tile([P, B * H], F32, name="recip")
-        nc.vector.reciprocal(out=recip[:], in_=denom_all[:])
+
+        def spread_denom():
+            denom_ps = psum.tile([P, P], BF16, name="bank")
+            nc.tensor.transpose(denom_ps[:], denom_col[:, 0:1].to_broadcast([P, P]), ident[:])
+            nc.vector.reciprocal(out=recip[:], in_=denom_ps[:, 0 : B * H])
 
         bias = keep.tile([P, E], BF16, name="bias")
 
         def spread_bias():
-            bias_ps = psum.tile([P, E // P, P], BF16, name="bank")
-            for c in range(E // P):
-                nc.tensor.transpose(bias_ps[:, c, :], bo_cols[:, c : c + 1].to_broadcast([P, P]), ident[:])
+            bias_ps = psum.tile([P, E], F32, name="bank")
+            nc.tensor.matmul(bias_ps[:], lhsT=ones[:], rhs=bias_row[:], start=True, stop=True)
             return bias_ps
 
         def copy_bias(engine, bias_ps):
-            copy(engine, bias[:].rearrange("m (p c) -> m p c", p=P), bias_ps[:].rearrange("m c p -> m p c"))
+            copy(engine, bias[:], bias_ps[:])
 
         t_ps = {}
         c_ps = {}
@@ -104,7 +111,7 @@ def tile_linearattention_pb_s_kernel(tc, q_feat, kv, denom, Wo, bo, out):
         for b in range(B):
             for g in range(PASSES):
                 q_t[b, g] = keep.tile([P, PACK, ROWS, RUNS], BF16, name="q_t%d%d" % (b, g))
-                c_sb[b, g] = keep.tile([P, PACK * DH], BF16, name="c_sb%d%d" % (b, g), align_bytes=64)
+                c_sb[b, g] = keep.tile([P, PAIRS, PACK, DH // PAIRS], BF16, name="c_sb%d%d" % (b, g), align_bytes=64)
         grouped = [keep.tile([P, PASSES, S, PACK], BF16, name="grouped%d" % b, align_bytes=64) for b in range(B)]
         codes = [keep.tile([P, PASSES * S], U32, name="codes%d" % b, align_bytes=64) for b in range(B)]
         scales = [keep.tile([P, PASSES * S], U8, name="scales%d" % b, align_bytes=64) for b in range(B)]
@@ -129,12 +136,12 @@ def tile_linearattention_pb_s_kernel(tc, q_feat, kv, denom, Wo, bo, out):
             copy(engine, q_t[b, g][:], t_ps[b, g][:].rearrange("d j (t u) -> d t j u", u=RUNS))
 
         def first_matmul(b, g):
-            c_ps[b, g] = psum.tile([P, PACK, DH], F32, name="bank")
+            c_ps[b, g] = psum.tile([P, PAIRS, PACK, DH // PAIRS], F32, name="bank")
             for t in range(PACK):
                 nc.tensor.matmul(
-                    c_ps[b, g][:, t, :],
+                    c_ps[b, g][:, :, t, :].rearrange("s w (r i) -> s w r i", i=2),
                     lhsT=q_t[b, g][:, t, :, :].rearrange("d j u -> d (j u)"),
-                    rhs=kv_sb[b][:, g * PACK + t, :],
+                    rhs=kv_sb[b][:, g * PACK + t, :].rearrange("d (r w i) -> d w r i", w=PAIRS, i=2),
                     start=True,
                     stop=True,
                 )
@@ -144,24 +151,24 @@ def tile_linearattention_pb_s_kernel(tc, q_feat, kv, denom, Wo, bo, out):
             if engine is nc.scalar:
                 for t in range(PACK):
                     nc.scalar.activation(
-                        out=c_sb[b, g][:, t * DH : (t + 1) * DH],
-                        in_=c_ps[b, g][:, t, :],
+                        out=c_sb[b, g][:, :, t, :],
+                        in_=c_ps[b, g][:, :, t, :],
                         func=COPY,
                         scale=recip[:, first + t : first + t + 1],
                     )
             else:
                 nc.vector.tensor_tensor(
-                    out=c_sb[b, g][:].rearrange("p (t e) -> p t e", t=PACK),
+                    out=c_sb[b, g][:],
                     in0=c_ps[b, g][:],
-                    in1=recip[:, first : first + PACK].unsqueeze(2).to_broadcast([P, PACK, DH]),
+                    in1=recip[:, first : first + PACK].unsqueeze(1).unsqueeze(3).to_broadcast([P, PAIRS, PACK, DH // PAIRS]),
                     op=MULT,
                 )
 
         def transpose_c(b, g):
-            w_ps[b, g] = psum.tile([P, 2, S], F32, name="bank")
-            words = c_sb[b, g][:].bitcast(F32)
-            for u in range(2):
-                nc.tensor.transpose(w_ps[b, g][:, u, :], words[:, u::2], ident_words[:])
+            w_ps[b, g] = psum.tile([P, PAIRS, S], F32, name="bank")
+            for w in range(PAIRS):
+                words = c_sb[b, g][:, w, :, :].rearrange("s t x -> s (t x)").bitcast(F32)
+                nc.tensor.transpose(w_ps[b, g][:, w, :], words, ident_words[:])
 
         def copy_c(engine, b, g):
             copy(
@@ -220,42 +227,43 @@ def tile_linearattention_pb_s_kernel(tc, q_feat, kv, denom, Wo, bo, out):
         S_, V_, G_ = nc.scalar, nc.vector, nc.gpsimd
         transpose_q(0, 0)
         copy_q(V_, 0, 0)
+        spread_denom()
         transpose_q(0, 1)
         first_matmul(0, 0)
         copy_q(V_, 0, 1)
-        bias_ps = spread_bias()
         divide(V_, 0, 0)
         first_matmul(0, 1)
-        copy_bias(S_, bias_ps)
         transpose_q(1, 0)
         divide(V_, 0, 1)
-        group_wo(G_, 0, HALF, 384)
+        group_wo(G_, 0, HALF, E)
         transpose_q(1, 1)
         copy_q(S_, 1, 0)
         group_wo(V_, 0, 0, HALF)
         transpose_c(0, 0)
         transpose_c(0, 1)
         copy_q(S_, 1, 1)
-        group_wo(V_, 0, 384, E)
+        quantise_wo(0, 0, HALF)
         first_matmul(1, 0)
         copy_c(S_, 0, 0)
         first_matmul(1, 1)
         divide(V_, 1, 0)
         copy_c(S_, 0, 1)
+        bias_ps = spread_bias()
         group_wo(G_, 1, HALF, 384)
         divide(S_, 1, 1)
-        quantise_wo(0, 0, E)
+        quantise_wo(0, HALF, E)
         transpose_c(1, 0)
-        group_wo(S_, 1, 384, E)
         group_wo(V_, 1, 0, HALF)
+        group_wo(S_, 1, 384, E)
         transpose_c(1, 1)
-        copy_c(S_, 1, 0)
         quantise_c(0)
-        copy_c(S_, 1, 1)
+        copy_c(S_, 1, 0)
         quantise_wo(1, 0, HALF)
+        copy_c(S_, 1, 1)
         second_matmul(0, 0, 0, HALF)
         quantise_wo(1, HALF, E)
         second_matmul(0, 0, HALF, E)
+        copy_bias(S_, bias_ps)
         quantise_c(1)
         second_matmul(0, 1, 0, HALF)
         second_matmul(0, 1, HALF, E)

@@ -61,14 +61,11 @@ def tile_linearattention_pb_s_kernel(tc, q_feat, kv, denom, Wo, bo, out):
             nc.scalar.dma_start(out=denom_col[0 : B * H, 0:1], in_=denom.rearrange("b h x y -> (b h) (x y)"))
 
         def load_bo():
-            nc.scalar.dma_start(out=bias_row[0:1, :], in_=bo.unsqueeze(0))
+            nc.scalar.dma_start(out=bo_cols[:], in_=bo.rearrange("(p c) -> p c", p=P))
 
         denom_col = keep.tile([P, 2], BF16, name="denom_col")
         nc.vector.memset(denom_col[:], 0.0)
-        bias_row = keep.tile([P, E], BF16, name="bias_row")
-        nc.vector.memset(bias_row[:], 0.0)
-        ones = keep.tile([P, P], BF16, name="ones")
-        nc.vector.memset(ones[:], 1.0)
+        bo_cols = keep.tile([P, E // P], BF16, name="bo_cols")
         load_q(0, 0)
         load_denom()
         load_bo()
@@ -93,15 +90,20 @@ def tile_linearattention_pb_s_kernel(tc, q_feat, kv, denom, Wo, bo, out):
             nc.tensor.transpose(denom_ps[:], denom_col[:, 0:1].to_broadcast([P, P]), ident[:])
             nc.vector.reciprocal(out=recip[:], in_=denom_ps[:, 0 : B * H])
 
+        def keep_busy():
+            busy_ps = psum.tile([P, P], F32, name="bank")
+            nc.tensor.matmul(busy_ps[:], lhsT=ident_words[:], rhs=ident_words[:], start=True, stop=True)
+
         bias = keep.tile([P, E], BF16, name="bias")
 
         def spread_bias():
-            bias_ps = psum.tile([P, E], F32, name="bank")
-            nc.tensor.matmul(bias_ps[:], lhsT=ones[:], rhs=bias_row[:], start=True, stop=True)
+            bias_ps = psum.tile([P, E // P, P], BF16, name="bank")
+            for c in range(E // P):
+                nc.tensor.transpose(bias_ps[:, c, :], bo_cols[:, c : c + 1].to_broadcast([P, P]), ident[:])
             return bias_ps
 
         def copy_bias(engine, bias_ps):
-            copy(engine, bias[:], bias_ps[:])
+            copy(engine, bias[:].rearrange("m (p c) -> m p c", p=P), bias_ps[:].rearrange("m c p -> m p c"))
 
         t_ps = {}
         c_ps = {}
@@ -225,11 +227,15 @@ def tile_linearattention_pb_s_kernel(tc, q_feat, kv, denom, Wo, bo, out):
             nc.sync.dma_start(out=out[b][:, lo:hi], in_=result[:])
 
         S_, V_, G_ = nc.scalar, nc.vector, nc.gpsimd
+        keep_busy()
+        keep_busy()
         transpose_q(0, 0)
         copy_q(V_, 0, 0)
         spread_denom()
+        keep_busy()
         transpose_q(0, 1)
         first_matmul(0, 0)
+        keep_busy()
         copy_q(V_, 0, 1)
         divide(V_, 0, 0)
         first_matmul(0, 1)

from contextlib import ExitStack

import concourse.mybir as mybir
from concourse.masks import make_identity

BF16 = mybir.dt.bfloat16
F32 = mybir.dt.float32
U32 = mybir.dt.uint32
U8 = mybir.dt.uint8
FP8X4 = mybir.dt.float8_e4m3fn_x4
MULT = mybir.AluOpType.mult
ADD = mybir.AluOpType.add
COPY = mybir.ActivationFunctionType.Copy

P = 128
B = 2
H = 8
S = 128
DH = 128
E = 512
PACK = 4
PAIRS = 2
PASSES = H // PACK
HALF = E // 2
ROWS = 4
RUNS = S // ROWS

FLOPS = 2 * B * H * S * DH * DH + 2 * B * S * H * DH * E


def tile_linearattention_pb_s_kernel(tc, q_feat, kv, denom, Wo, bo, out):
    nc = tc.nc
    with ExitStack() as ctx:
        keep = ctx.enter_context(tc.tile_pool(name="keep", bufs=1))
        psum = ctx.enter_context(tc.psum_pool(name="psum", bufs=8))
        ctx.enter_context(tc.manual_schedule())

        q_rows = [keep.tile([P, PASSES, ROWS, DH], BF16, name="q_rows%d" % b) for b in range(B)]
        kv_sb = [keep.tile([P, H, DH], BF16, name="kv_sb%d" % b) for b in range(B)]
        wo_raw = [keep.tile([P, PACK, E], BF16, name="wo_raw%d" % g) for g in range(PASSES)]
        wo_view = Wo.rearrange("(g p t) n -> g p t n", t=PACK, p=P)

        def load_q(b, g=None):
            if g is None:
                view = q_feat[b].rearrange("(g t) (u j) d -> (t u) g j d", t=PACK, j=ROWS)
                nc.sync.dma_start(out=q_rows[b][:], in_=view)
            else:
                heads = slice(g * PACK, (g + 1) * PACK)
                view = q_feat[b, heads].rearrange("t (u j) d -> (t u) j d", j=ROWS)
                nc.sync.dma_start(out=q_rows[b][:, g, :, :], in_=view)

        def load_kv(b, g=None):
            heads = slice(0, H) if g is None else slice(g * PACK, (g + 1) * PACK)
            nc.sync.dma_start(out=kv_sb[b][:, heads, :], in_=kv[b, heads].rearrange("h d e -> d h e"))

        def load_wo(g, half=None):
            cols = slice(0, E) if half is None else slice(half * HALF, (half + 1) * HALF)
            nc.sync.dma_start(out=wo_raw[g][:, :, cols], in_=wo_view[g][:, :, cols])

        def load_denom():
            nc.scalar.dma_start(out=denom_col[0 : B * H, 0:1], in_=denom.rearrange("b h x y -> (b h) (x y)"))

        def load_bo():
            nc.scalar.dma_start(out=bo_cols[:], in_=bo.rearrange("(p c) -> p c", p=P))

        denom_col = keep.tile([P, 2], BF16, name="denom_col")
        nc.vector.memset(denom_col[:], 0.0)
        bo_cols = keep.tile([P, E // P], BF16, name="bo_cols")
        load_q(0, 0)
        load_denom()
        load_bo()
        load_kv(0, 0)
        load_q(0, 1)
        load_kv(0, 1)
        load_q(1)
        load_wo(0)
        load_kv(1, 0)
        load_kv(1, 1)
        load_wo(1)

        ident = keep.tile([P, P], BF16, name="ident")
        make_identity(nc, ident[:])
        ident_words = keep.tile([P, P], F32, name="ident_words")
        nc.vector.tensor_copy(out=ident_words[:], in_=ident[:])

        recip = keep.tile([P, B * H], F32, name="recip")

        def spread_denom():
            denom_ps = psum.tile([P, P], BF16, name="bank")
            nc.tensor.transpose(denom_ps[:], denom_col[:, 0:1].to_broadcast([P, P]), ident[:])
            nc.vector.reciprocal(out=recip[:], in_=denom_ps[:, 0 : B * H])

        def keep_busy():
            busy_ps = psum.tile([P, P], F32, name="bank")
            nc.tensor.matmul(busy_ps[:], lhsT=ident_words[:], rhs=ident_words[:], start=True, stop=True)

        bias = keep.tile([P, E], BF16, name="bias")

        def spread_bias():
            bias_ps = psum.tile([P, E // P, P], BF16, name="bank")
            for c in range(E // P):
                nc.tensor.transpose(bias_ps[:, c, :], bo_cols[:, c : c + 1].to_broadcast([P, P]), ident[:])
            return bias_ps

        def copy_bias(engine, bias_ps):
            copy(engine, bias[:].rearrange("m (p c) -> m p c", p=P), bias_ps[:].rearrange("m c p -> m p c"))

        t_ps = {}
        c_ps = {}
        w_ps = {}
        q_t = {}
        c_sb = {}
        for b in range(B):
            for g in range(PASSES):
                q_t[b, g] = keep.tile([P, PACK, ROWS, RUNS], BF16, name="q_t%d%d" % (b, g))
                c_sb[b, g] = keep.tile([P, PAIRS, PACK, DH // PAIRS], BF16, name="c_sb%d%d" % (b, g), align_bytes=64)
        grouped = [keep.tile([P, PASSES, S, PACK], BF16, name="grouped%d" % b, align_bytes=64) for b in range(B)]
        codes = [keep.tile([P, PASSES * S], U32, name="codes%d" % b, align_bytes=64) for b in range(B)]
        scales = [keep.tile([P, PASSES * S], U8, name="scales%d" % b, align_bytes=64) for b in range(B)]
        wo_grouped = [keep.tile([P, E, PACK], BF16, name="wo_grouped%d" % g, align_bytes=64) for g in range(PASSES)]
        wo_codes = [keep.tile([P, E], U32, name="wo_codes%d" % g, align_bytes=64) for g in range(PASSES)]
        wo_scales = [keep.tile([P, E], U8, name="wo_scales%d" % g, align_bytes=64) for g in range(PASSES)]

        def copy(engine, out, in_):
            if engine is nc.scalar:
                nc.scalar.copy(out=out, in_=in_)
            elif engine is nc.gpsimd:
                nc.gpsimd.tensor_scalar(out=out, in0=in_, scalar1=1.0, scalar2=0.0, op0=MULT, op1=ADD)
            else:
                engine.tensor_copy(out=out, in_=in_)

        def transpose_q(b, g):
            t_ps[b, g] = psum.tile([P, ROWS, P], BF16, name="bank")
            for j in range(ROWS):
                nc.tensor.transpose(t_ps[b, g][:, j, :], q_rows[b][:, g, j, :], ident[:])

        def copy_q(engine, b, g):
            copy(engine, q_t[b, g][:], t_ps[b, g][:].rearrange("d j (t u) -> d t j u", u=RUNS))

        def first_matmul(b, g):
            c_ps[b, g] = psum.tile([P, PAIRS, PACK, DH // PAIRS], F32, name="bank")
            for t in range(PACK):
                nc.tensor.matmul(
                    c_ps[b, g][:, :, t, :].rearrange("s w (r i) -> s w r i", i=2),
                    lhsT=q_t[b, g][:, t, :, :].rearrange("d j u -> d (j u)"),
                    rhs=kv_sb[b][:, g * PACK + t, :].rearrange("d (r w i) -> d w r i", w=PAIRS, i=2),
                    start=True,
                    stop=True,
                )

        def divide(engine, b, g):
            first = b * H + g * PACK
            if engine is nc.scalar:
                for t in range(PACK):
                    nc.scalar.activation(
                        out=c_sb[b, g][:, :, t, :],
                        in_=c_ps[b, g][:, :, t, :],
                        func=COPY,
                        scale=recip[:, first + t : first + t + 1],
                    )
            else:
                nc.vector.tensor_tensor(
                    out=c_sb[b, g][:],
                    in0=c_ps[b, g][:],
                    in1=recip[:, first : first + PACK].unsqueeze(1).unsqueeze(3).to_broadcast([P, PAIRS, PACK, DH // PAIRS]),
                    op=MULT,
                )

        def transpose_c(b, g):
            w_ps[b, g] = psum.tile([P, PAIRS, S], F32, name="bank")
            for w in range(PAIRS):
                words = c_sb[b, g][:, w, :, :].rearrange("s t x -> s (t x)").bitcast(F32)
                nc.tensor.transpose(w_ps[b, g][:, w, :], words, ident_words[:])

        def copy_c(engine, b, g):
            copy(
                engine,
                grouped[b][:, g, :, :].rearrange("p s t -> p (s t)").bitcast(F32).rearrange("p (u j w) -> p u j w", j=ROWS, w=2),
                w_ps[b, g][:].rearrange("p w (j u) -> p u j w", j=ROWS),
            )

        def quantise_c(b, g=None):
            lo, hi = (0, PASSES) if g is None else (g, g + 1)
            nc.vector.quantize_mx(
                out=codes[b][:, lo * S : hi * S].bitcast(FP8X4),
                scales=scales[b][:, lo * S : hi * S],
                in_=grouped[b][:, lo:hi, :, :].rearrange("p g s t -> p (g s t)"),
            )

        def group_wo(engine, g, lo, hi):
            dst = wo_grouped[g][:, lo:hi, :]
            src = wo_raw[g][:, :, lo:hi]
            if engine is nc.gpsimd:
                copy(engine, dst, src.rearrange("p t n -> p n t"))
            else:
                copy(
                    engine,
                    dst.rearrange("p (c i) t -> p c t i", i=4),
                    src.rearrange("p t (c i) -> p c t i", i=4),
                )

        def quantise_wo(g, lo, hi):
            nc.vector.quantize_mx(
                out=wo_codes[g][:, lo:hi].bitcast(FP8X4),
                scales=wo_scales[g][:, lo:hi],
                in_=wo_grouped[g][:, lo:hi, :].rearrange("p n t -> p (n t)"),
            )

        o_ps = {}

        def second_matmul(b, g, lo, hi):
            if g == 0:
                o_ps[b, lo] = psum.tile([P, hi - lo], F32, name="bank")
            nc.tensor.matmul_mx(
                out=o_ps[b, lo][:],
                lhsT=codes[b][:, g * S : (g + 1) * S].bitcast(FP8X4),
                lhsT_scale=scales[b][:, g * S : (g + 1) * S],
                rhs=wo_codes[g][:, lo:hi].bitcast(FP8X4),
                rhs_scale=wo_scales[g][:, lo:hi],
                start=(g == 0),
                stop=(g == PASSES - 1),
            )

        def finish(b, lo, hi):
            result = keep.tile([P, hi - lo], F32, name="result%d%d" % (b, lo))
            nc.vector.tensor_tensor(out=result[:], in0=o_ps[b, lo][:], in1=bias[:, lo:hi], op=ADD)
            nc.sync.dma_start(out=out[b][:, lo:hi], in_=result[:])

        S_, V_, G_ = nc.scalar, nc.vector, nc.gpsimd
        keep_busy()
        keep_busy()
        transpose_q(0, 0)
        copy_q(V_, 0, 0)
        spread_denom()
        keep_busy()
        transpose_q(0, 1)
        first_matmul(0, 0)
        keep_busy()
        copy_q(V_, 0, 1)
        divide(V_, 0, 0)
        first_matmul(0, 1)
        transpose_q(1, 0)
        divide(V_, 0, 1)
        group_wo(G_, 0, HALF, E)
        transpose_q(1, 1)
        copy_q(S_, 1, 0)
        group_wo(V_, 0, 0, HALF)
        transpose_c(0, 0)
        transpose_c(0, 1)
        copy_q(S_, 1, 1)
        quantise_wo(0, 0, HALF)
        first_matmul(1, 0)
        copy_c(S_, 0, 0)
        first_matmul(1, 1)
        divide(V_, 1, 0)
        copy_c(S_, 0, 1)
        bias_ps = spread_bias()
        group_wo(G_, 1, HALF, 384)
        divide(S_, 1, 1)
        quantise_wo(0, HALF, E)
        transpose_c(1, 0)
        group_wo(V_, 1, 0, HALF)
        group_wo(S_, 1, 384, E)
        transpose_c(1, 1)
        quantise_c(0)
        copy_c(S_, 1, 0)
        quantise_wo(1, 0, HALF)
        copy_c(S_, 1, 1)
        second_matmul(0, 0, 0, HALF)
        quantise_wo(1, HALF, E)
        second_matmul(0, 0, HALF, E)
        copy_bias(S_, bias_ps)
        quantise_c(1)
        second_matmul(0, 1, 0, HALF)
        second_matmul(0, 1, HALF, E)
        finish(0, 0, HALF)
        second_matmul(1, 0, 0, HALF)
        second_matmul(1, 1, 0, HALF)
        finish(0, HALF, E)
        second_matmul(1, 0, HALF, E)
        second_matmul(1, 1, HALF, E)
        finish(1, 0, HALF)
        finish(1, HALF, E)
